import numpy as np
import ml_dtypes


def mxq(x, axis, fmt="e4m3"):
    dtype, down = {"e4m3": (ml_dtypes.float8_e4m3fn, 7), "e5m2": (ml_dtypes.float8_e5m2, 14)}[fmt]
    v = np.moveaxis(np.asarray(x, np.float32).astype(ml_dtypes.bfloat16).astype(np.float64), axis, -1)
    blocks = v.reshape(v.shape[:-1] + (-1, 32))
    amax = np.abs(blocks).max(-1, keepdims=True)
    byte = np.maximum(np.where(amax > 0, np.frexp(amax)[1] - 1 + 127, 0) - down, 1)
    scale = np.exp2(byte - 127.0)
    codes = (blocks / scale).astype(np.float32).astype(dtype).astype(np.float64)
    return np.moveaxis((codes * scale).reshape(v.shape), -1, axis)


WIDE = False


def mx_kscale(k):
    if not WIDE:
        return np.ones(k)
    levels = np.array([10, -10, 5, -5, 0])
    a = np.random.permutation(np.resize(levels, k // 512 * 4)).reshape(k // 512, 4)
    idx = np.arange(k)
    return np.exp2(a[idx // 512, idx % 128 // 32])


BF16 = ml_dtypes.bfloat16


def bf(x):
    return np.asarray(x, np.float32).astype(BF16)


def f64(x):
    return np.asarray(x).astype(np.float64)


B, S, IN, OUT, SP = 4, 32, 4096, 4096, 640


def setup_inputs():
    s = mx_kscale(IN)
    return {"x": bf(np.random.standard_normal((B, S, IN)) * s),
            "weights": bf(np.random.standard_normal((OUT, IN)) / np.sqrt(IN) / s[None, :])}


def reference(x, weights):
    x = f64(x)
    weights = f64(weights)
    size_out = x.shape[:-1] + (OUT,)
    xf = x.reshape(-1, x.shape[-1])
    xq = mxq(xf, 1, "e4m3")
    w_sparse = weights[:SP, :]
    w_dense = weights[SP:, :]
    out_sparse = xq @ mxq(w_sparse, 1, "e4m3").T
    out_dense = xq @ mxq(w_dense, 1, "e4m3").T
    out = np.concatenate([out_sparse, out_dense], axis=1)
    return out.reshape(size_out)

@@ -1,0 +1,123 @@
+from contextlib import ExitStack
+
+import concourse.mybir as mybir
+from concourse.masks import make_identity
+
+BF16 = mybir.dt.bfloat16
+F32 = mybir.dt.float32
+U32 = mybir.dt.uint32
+U8 = mybir.dt.uint8
+FP8X4 = mybir.dt.float8_e4m3fn_x4
+
+P = 128
+K = 4096
+OUT = 4096
+PASSES = K // 512
+CHUNKS = OUT // P
+AHEAD = 8
+FLOPS = 2 * P * K * OUT
+
+
+def tile_myinterleavedmodule_kernel(tc, x, weights, out):
+    nc = tc.nc
+    xf = x.flatten_outer_dims()
+    of = out.flatten_outer_dims()
+    with ExitStack() as ctx:
+        const = ctx.enter_context(tc.tile_pool(name="const", bufs=1))
+        raw = ctx.enter_context(tc.tile_pool(name="raw", bufs=AHEAD))
+        grp = ctx.enter_context(tc.tile_pool(name="grp", bufs=3))
+        qnt = ctx.enter_context(tc.tile_pool(name="qnt", bufs=3))
+        res = ctx.enter_context(tc.tile_pool(name="res", bufs=3))
+        tps = ctx.enter_context(tc.psum_pool(name="tps", bufs=6))
+        aps = ctx.enter_context(tc.psum_pool(name="aps", bufs=2))
+        ctx.enter_context(tc.manual_schedule())
+
+        ident = const.tile([P, P], F32, name="ident")
+        make_identity(nc, ident[:])
+
+        def load(rows, pool, name):
+            t = pool.tile([P, K], BF16, name=name)
+            nc.sync.dma_start(out=t[:], in_=rows)
+            return t
+
+        def transposes(t):
+            words = t[:].bitcast(F32)
+            banks = []
+            for b in range(4):
+                bank = tps.tile([P, 4, P], F32, name="bank")
+                for j in range(4):
+                    w0 = (4 * b + j) * P
+                    nc.tensor.transpose(bank[:, j, :], words[:, w0 : w0 + P], ident[:])
+                banks.append(bank)
+            return banks
+
+        def regroup(copy, bank, grouped, b):
+            dst = grouped[:].bitcast(F32).rearrange("p (g r u) -> p g r u", g=PASSES, u=2)
+            copy(out=dst[:, 2 * b : 2 * b + 2, :, :], in_=bank[:].rearrange("p (g u) r -> p g r u", u=2))
+
+        def quantise(grouped, codes, scales, h):
+            c0 = h * 512
+            nc.vector.quantize_mx(
+                out=codes[:, c0 : c0 + 512].bitcast(FP8X4),
+                scales=scales[:, c0 : c0 + 512],
+                in_=grouped[:, 4 * c0 : 4 * c0 + 2048],
+            )
+
+        x_sb = load(xf, const, "x_sb")
+        w_sb = {}
+        for c in range(AHEAD):
+            w_sb[c] = load(weights[c * P : (c + 1) * P, :], raw, "w_sb")
+
+        x_banks = transposes(x_sb)
+        x_grouped = grp.tile([P, K], BF16, name="grouped", align_bytes=64)
+        x_codes = const.tile([P, PASSES * P], U32, name="x_codes", align_bytes=64)
+        x_scales = const.tile([P, PASSES * P], U8, name="x_scales", align_bytes=64)
+        regroup(nc.scalar.copy, x_banks[0], x_grouped, 0)
+        regroup(nc.vector.tensor_copy, x_banks[1], x_grouped, 1)
+        regroup(nc.scalar.copy, x_banks[2], x_grouped, 2)
+        regroup(nc.vector.tensor_copy, x_banks[3], x_grouped, 3)
+        quantise(x_grouped, x_codes, x_scales, 0)
+        quantise(x_grouped, x_codes, x_scales, 1)
+
+        w_q = {}
+        acc = {}
+        for c in range(CHUNKS + 1):
+            if c < CHUNKS:
+                banks = transposes(w_sb[c])
+                if c + AHEAD < CHUNKS:
+                    n = c + AHEAD
+                    w_sb[n] = load(weights[n * P : (n + 1) * P, :], raw, "w_sb")
+            if c >= 1:
+                m = c - 1
+                if m % 4 == 0:
+                    acc[m // 4] = aps.tile([P, 512], F32, name="acc")
+                codes, scales = w_q[m]
+                col = (m % 4) * P
+                for g in range(PASSES):
+                    s = slice(g * P, (g + 1) * P)
+                    nc.tensor.matmul_mx(
+                        out=acc[m // 4][:, col : col + P],
+                        lhsT=x_codes[:, s].bitcast(FP8X4),
+                        lhsT_scale=x_scales[:, s],
+                        rhs=codes[:, s].bitcast(FP8X4),
+                        rhs_scale=scales[:, s],
+                        start=(g == 0),
+                        stop=(g == PASSES - 1),
+                    )
+            if c < CHUNKS:
+                grouped = grp.tile([P, K], BF16, name="grouped", align_bytes=64)
+                codes = qnt.tile([P, PASSES * P], U32, name="codes", align_bytes=64)
+                scales = qnt.tile([P, PASSES * P], U8, name="scales", align_bytes=64)
+                w_q[c] = (codes, scales)
+                regroup(nc.scalar.copy, banks[0], grouped, 0)
+                regroup(nc.scalar.copy, banks[1], grouped, 1)
+                regroup(nc.scalar.copy, banks[2], grouped, 2)
+                regroup(nc.vector.tensor_copy, banks[3], grouped, 3)
+                quantise(grouped, codes, scales, 0)
+                quantise(grouped, codes, scales, 1)
+            if c >= 1 and (c - 1) % 4 == 3:
+                n = (c - 1) // 4
+                o_sb = res.tile([P, 512], F32, name="o_sb")
+                nc.scalar.copy(out=o_sb[:], in_=acc[n][:])
+                queue = nc.sync if c == CHUNKS else nc.scalar
+                queue.dma_start(out=of[:, n * 512 : (n + 1) * 512], in_=o_sb[:])

@@ -14,7 +14,10 @@ K = 4096
 OUT = 4096
 PASSES = K // 512
 CHUNKS = OUT // P
-AHEAD = 8
+LAST = CHUNKS - 1
+AHEAD = 12
+RUN = 1
+LATE_FROM = 3
 FLOPS = 2 * P * K * OUT
 
 
@@ -26,98 +29,142 @@ def tile_myinterleavedmodule_kernel(tc, x, weights, out):
         const = ctx.enter_context(tc.tile_pool(name="const", bufs=1))
         raw = ctx.enter_context(tc.tile_pool(name="raw", bufs=AHEAD))
         grp = ctx.enter_context(tc.tile_pool(name="grp", bufs=3))
-        qnt = ctx.enter_context(tc.tile_pool(name="qnt", bufs=3))
-        res = ctx.enter_context(tc.tile_pool(name="res", bufs=3))
+        qnt = ctx.enter_context(tc.tile_pool(name="qnt", bufs=5))
         tps = ctx.enter_context(tc.psum_pool(name="tps", bufs=6))
         aps = ctx.enter_context(tc.psum_pool(name="aps", bufs=2))
         ctx.enter_context(tc.manual_schedule())
 
         ident = const.tile([P, P], F32, name="ident")
         make_identity(nc, ident[:])
+        o_sb = const.tile([P, OUT], F32, name="o_sb")
 
-        def load(rows, pool, name):
+        def load(rows, pool, name, pieces):
             t = pool.tile([P, K], BF16, name=name)
-            nc.sync.dma_start(out=t[:], in_=rows)
+            w = K // pieces
+            for i in range(pieces):
+                nc.sync.dma_start(out=t[:, i * w : (i + 1) * w], in_=rows[:, i * w : (i + 1) * w])
             return t
 
-        def transposes(t):
+        def load_chunk(c):
+            pieces = 4 if c in (0, LAST) else 1
+            return load(weights[c * P : (c + 1) * P, :], raw, "w_sb", pieces)
+
+        def transposes(t, g0, ng):
             words = t[:].bitcast(F32)
-            banks = []
-            for b in range(4):
-                bank = tps.tile([P, 4, P], F32, name="bank")
-                for j in range(4):
-                    w0 = (4 * b + j) * P
-                    nc.tensor.transpose(bank[:, j, :], words[:, w0 : w0 + P], ident[:])
-                banks.append(bank)
-            return banks
+            bank = tps.tile([P, 2 * ng, P], F32, name="bank")
+            for j in range(2 * ng):
+                w0 = (2 * g0 + j) * P
+                nc.tensor.transpose(bank[:, j, :], words[:, w0 : w0 + P], ident[:])
+            return bank
 
-        def regroup(copy, bank, grouped, b):
+        def regroup(copy, bank, grouped, g0, ng):
             dst = grouped[:].bitcast(F32).rearrange("p (g r u) -> p g r u", g=PASSES, u=2)
-            copy(out=dst[:, 2 * b : 2 * b + 2, :, :], in_=bank[:].rearrange("p (g u) r -> p g r u", u=2))
+            copy(out=dst[:, g0 : g0 + ng, :, :], in_=bank[:].rearrange("p (g u) r -> p g r u", u=2))
 
-        def quantise(grouped, codes, scales, h):
-            c0 = h * 512
+        def quantise(grouped, codes, scales, g0, ng):
+            c0 = g0 * P
+            c1 = c0 + ng * P
             nc.vector.quantize_mx(
-                out=codes[:, c0 : c0 + 512].bitcast(FP8X4),
-                scales=scales[:, c0 : c0 + 512],
-                in_=grouped[:, 4 * c0 : 4 * c0 + 2048],
+                out=codes[:, c0:c1].bitcast(FP8X4),
+                scales=scales[:, c0:c1],
+                in_=grouped[:, 4 * c0 : 4 * c1],
             )
 
-        x_sb = load(xf, const, "x_sb")
+        x_sb = load(xf, const, "x_sb", 4)
         w_sb = {}
         for c in range(AHEAD):
-            w_sb[c] = load(weights[c * P : (c + 1) * P, :], raw, "w_sb")
+            w_sb[c] = load_chunk(c)
 
-        x_banks = transposes(x_sb)
+        x_banks = [transposes(x_sb, 2 * b, 2) for b in range(4)]
         x_grouped = grp.tile([P, K], BF16, name="grouped", align_bytes=64)
         x_codes = const.tile([P, PASSES * P], U32, name="x_codes", align_bytes=64)
         x_scales = const.tile([P, PASSES * P], U8, name="x_scales", align_bytes=64)
-        regroup(nc.scalar.copy, x_banks[0], x_grouped, 0)
-        regroup(nc.vector.tensor_copy, x_banks[1], x_grouped, 1)
-        regroup(nc.scalar.copy, x_banks[2], x_grouped, 2)
-        regroup(nc.vector.tensor_copy, x_banks[3], x_grouped, 3)
-        quantise(x_grouped, x_codes, x_scales, 0)
-        quantise(x_grouped, x_codes, x_scales, 1)
+        regroup(nc.scalar.copy, x_banks[0], x_grouped, 0, 2)
+        regroup(nc.vector.tensor_copy, x_banks[1], x_grouped, 2, 2)
+        regroup(nc.scalar.copy, x_banks[2], x_grouped, 4, 2)
+        regroup(nc.vector.tensor_copy, x_banks[3], x_grouped, 6, 2)
+        quantise(x_grouped, x_codes, x_scales, 0, 4)
+        quantise(x_grouped, x_codes, x_scales, 4, 4)
 
         w_q = {}
         acc = {}
-        for c in range(CHUNKS + 1):
-            if c < CHUNKS:
-                banks = transposes(w_sb[c])
-                if c + AHEAD < CHUNKS:
-                    n = c + AHEAD
-                    w_sb[n] = load(weights[n * P : (n + 1) * P, :], raw, "w_sb")
-            if c >= 1:
-                m = c - 1
-                if m % 4 == 0:
-                    acc[m // 4] = aps.tile([P, 512], F32, name="acc")
-                codes, scales = w_q[m]
-                col = (m % 4) * P
-                for g in range(PASSES):
-                    s = slice(g * P, (g + 1) * P)
-                    nc.tensor.matmul_mx(
-                        out=acc[m // 4][:, col : col + P],
-                        lhsT=x_codes[:, s].bitcast(FP8X4),
-                        lhsT_scale=x_scales[:, s],
-                        rhs=codes[:, s].bitcast(FP8X4),
-                        rhs_scale=scales[:, s],
-                        start=(g == 0),
-                        stop=(g == PASSES - 1),
-                    )
-            if c < CHUNKS:
-                grouped = grp.tile([P, K], BF16, name="grouped", align_bytes=64)
-                codes = qnt.tile([P, PASSES * P], U32, name="codes", align_bytes=64)
-                scales = qnt.tile([P, PASSES * P], U8, name="scales", align_bytes=64)
-                w_q[c] = (codes, scales)
-                regroup(nc.scalar.copy, banks[0], grouped, 0)
-                regroup(nc.scalar.copy, banks[1], grouped, 1)
-                regroup(nc.scalar.copy, banks[2], grouped, 2)
-                regroup(nc.vector.tensor_copy, banks[3], grouped, 3)
-                quantise(grouped, codes, scales, 0)
-                quantise(grouped, codes, scales, 1)
-            if c >= 1 and (c - 1) % 4 == 3:
-                n = (c - 1) // 4
-                o_sb = res.tile([P, 512], F32, name="o_sb")
-                nc.scalar.copy(out=o_sb[:], in_=acc[n][:])
-                queue = nc.sync if c == CHUNKS else nc.scalar
-                queue.dma_start(out=of[:, n * 512 : (n + 1) * 512], in_=o_sb[:])
+        late = []
+
+        def multiply(m):
+            if m % 4 == 0 or m == LAST:
+                acc[m] = aps.tile([P, 512], F32, name="acc")
+                dst = acc[m][:, 0:P]
+            else:
+                dst = acc[m - m % 4][:, (m % 4) * P : (m % 4 + 1) * P]
+            codes, scales = w_q[m]
+            for g in range(PASSES):
+                s = slice(g * P, (g + 1) * P)
+                nc.tensor.matmul_mx(
+                    out=dst,
+                    lhsT=x_codes[:, s].bitcast(FP8X4),
+                    lhsT_scale=x_scales[:, s],
+                    rhs=codes[:, s].bitcast(FP8X4),
+                    rhs_scale=scales[:, s],
+                    start=(g == 0),
+                    stop=(g == PASSES - 1),
+                )
+
+        def finish(first, count):
+            cols = slice(first * P, (first + count) * P)
+            nc.scalar.copy(out=o_sb[:, cols], in_=acc[first][:, 0 : count * P])
+            if first // 4 < LATE_FROM:
+                nc.scalar.dma_start(out=of[:, cols], in_=o_sb[:, cols])
+            else:
+                late.append(cols)
+
+        loaded = AHEAD
+        multiplied = 0
+        sent = 0
+        for c in range(CHUNKS):
+            if c < LAST:
+                banks = [transposes(w_sb[c], 2 * b, 2) for b in range(4)]
+            else:
+                banks = [transposes(w_sb[c], 2 * b, 2) for b in range(3)]
+                banks.append(transposes(w_sb[c], 6, 1))
+                banks.append(transposes(w_sb[c], 7, 1))
+            if loaded < CHUNKS:
+                w_sb[loaded] = load_chunk(loaded)
+                loaded += 1
+            done = list(range(multiplied, c)) if (c % RUN == 0 or c == LAST) else []
+            for m in done:
+                multiply(m)
+            multiplied += len(done)
+            grouped = grp.tile([P, K], BF16, name="grouped", align_bytes=64)
+            codes = qnt.tile([P, PASSES * P], U32, name="codes", align_bytes=64)
+            scales = qnt.tile([P, PASSES * P], U8, name="scales", align_bytes=64)
+            w_q[c] = (codes, scales)
+            if c < LAST:
+                regroup(nc.scalar.copy, banks[0], grouped, 0, 2)
+                regroup(nc.scalar.copy, banks[1], grouped, 2, 2)
+                regroup(nc.scalar.copy, banks[2], grouped, 4, 2)
+                regroup(nc.vector.tensor_copy, banks[3], grouped, 6, 2)
+                quantise(grouped, codes, scales, 0, 4)
+                quantise(grouped, codes, scales, 4, 4)
+            else:
+                regroup(nc.scalar.copy, banks[0], grouped, 0, 2)
+                regroup(nc.vector.tensor_copy, banks[1], grouped, 2, 2)
+                regroup(nc.scalar.copy, banks[2], grouped, 4, 2)
+                quantise(grouped, codes, scales, 0, 2)
+                quantise(grouped, codes, scales, 2, 2)
+                regroup(nc.scalar.copy, banks[3], grouped, 6, 1)
+                regroup(nc.vector.tensor_copy, banks[4], grouped, 7, 1)
+                quantise(grouped, codes, scales, 4, 2)
+                quantise(grouped, codes, scales, 6, 2)
+            for m in done:
+                if m % 4 == 3:
+                    finish(m - 3, 4)
+                elif m == LAST - 1:
+                    finish(m - 2, 3)
+            if loaded == CHUNKS:
+                for cols in late[sent:]:
+                    nc.sync.dma_start(out=of[:, cols], in_=o_sb[:, cols])
+                sent = len(late)
+        multiply(LAST)
+        finish(LAST, 1)
+        for cols in late[sent:]:
+            nc.sync.dma_start(out=of[:, cols], in_=o_sb[:, cols])

@@ -16,7 +16,7 @@ PASSES = K // 512
 CHUNKS = OUT // P
 LAST = CHUNKS - 1
 AHEAD = 12
-RUN = 1
+RUN = 2
 LATE_FROM = 3
 FLOPS = 2 * P * K * OUT
 

@@ -16,7 +16,7 @@ PASSES = K // 512
 CHUNKS = OUT // P
 LAST = CHUNKS - 1
 AHEAD = 12
-RUN = 2
+RUN = 1
 LATE_FROM = 3
 FLOPS = 2 * P * K * OUT
 
@@ -111,9 +111,9 @@ def tile_myinterleavedmodule_kernel(tc, x, weights, out):
 
         def finish(first, count):
             cols = slice(first * P, (first + count) * P)
-            nc.scalar.copy(out=o_sb[:, cols], in_=acc[first][:, 0 : count * P])
+            nc.vector.tensor_copy(out=o_sb[:, cols], in_=acc[first][:, 0 : count * P])
             if first // 4 < LATE_FROM:
-                nc.scalar.dma_start(out=of[:, cols], in_=o_sb[:, cols])
+                nc.sync.dma_start(out=of[:, cols], in_=o_sb[:, cols])
             else:
                 late.append(cols)
 

@@ -16,7 +16,7 @@ PASSES = K // 512
 CHUNKS = OUT // P
 LAST = CHUNKS - 1
 AHEAD = 12
-RUN = 1
+LAG = 2
 LATE_FROM = 3
 FLOPS = 2 * P * K * OUT
 
@@ -111,9 +111,9 @@ def tile_myinterleavedmodule_kernel(tc, x, weights, out):
 
         def finish(first, count):
             cols = slice(first * P, (first + count) * P)
-            nc.vector.tensor_copy(out=o_sb[:, cols], in_=acc[first][:, 0 : count * P])
+            nc.scalar.copy(out=o_sb[:, cols], in_=acc[first][:, 0 : count * P])
             if first // 4 < LATE_FROM:
-                nc.sync.dma_start(out=of[:, cols], in_=o_sb[:, cols])
+                nc.scalar.dma_start(out=of[:, cols], in_=o_sb[:, cols])
             else:
                 late.append(cols)
 
@@ -130,7 +130,7 @@ def tile_myinterleavedmodule_kernel(tc, x, weights, out):
             if loaded < CHUNKS:
                 w_sb[loaded] = load_chunk(loaded)
                 loaded += 1
-            done = list(range(multiplied, c)) if (c % RUN == 0 or c == LAST) else []
+            done = list(range(multiplied, c if c >= LAST - 1 else c - LAG + 1))
             for m in done:
                 multiply(m)
             multiplied += len(done)

from contextlib import ExitStack

import concourse.mybir as mybir
from concourse.masks import make_identity

BF16 = mybir.dt.bfloat16
F32 = mybir.dt.float32
U32 = mybir.dt.uint32
U8 = mybir.dt.uint8
FP8X4 = mybir.dt.float8_e4m3fn_x4

P = 128
K = 4096
OUT = 4096
PASSES = K // 512
CHUNKS = OUT // P
LAST = CHUNKS - 1
AHEAD = 12
LAG = 2
LATE_FROM = 3
FLOPS = 2 * P * K * OUT


def tile_myinterleavedmodule_kernel(tc, x, weights, out):
    nc = tc.nc
    xf = x.flatten_outer_dims()
    of = out.flatten_outer_dims()
    with ExitStack() as ctx:
        const = ctx.enter_context(tc.tile_pool(name="const", bufs=1))
        raw = ctx.enter_context(tc.tile_pool(name="raw", bufs=AHEAD))
        grp = ctx.enter_context(tc.tile_pool(name="grp", bufs=3))
        qnt = ctx.enter_context(tc.tile_pool(name="qnt", bufs=5))
        tps = ctx.enter_context(tc.psum_pool(name="tps", bufs=6))
        aps = ctx.enter_context(tc.psum_pool(name="aps", bufs=2))
        ctx.enter_context(tc.manual_schedule())

        ident = const.tile([P, P], F32, name="ident")
        make_identity(nc, ident[:])
        o_sb = const.tile([P, OUT], F32, name="o_sb")

        def load(rows, pool, name, pieces):
            t = pool.tile([P, K], BF16, name=name)
            w = K // pieces
            for i in range(pieces):
                nc.sync.dma_start(out=t[:, i * w : (i + 1) * w], in_=rows[:, i * w : (i + 1) * w])
            return t

        def load_chunk(c):
            pieces = 4 if c in (0, LAST) else 1
            return load(weights[c * P : (c + 1) * P, :], raw, "w_sb", pieces)

        def transposes(t, g0, ng):
            words = t[:].bitcast(F32)
            bank = tps.tile([P, 2 * ng, P], F32, name="bank")
            for j in range(2 * ng):
                w0 = (2 * g0 + j) * P
                nc.tensor.transpose(bank[:, j, :], words[:, w0 : w0 + P], ident[:])
            return bank

        def regroup(copy, bank, grouped, g0, ng):
            dst = grouped[:].bitcast(F32).rearrange("p (g r u) -> p g r u", g=PASSES, u=2)
            copy(out=dst[:, g0 : g0 + ng, :, :], in_=bank[:].rearrange("p (g u) r -> p g r u", u=2))

        def quantise(grouped, codes, scales, g0, ng):
            c0 = g0 * P
            c1 = c0 + ng * P
            nc.vector.quantize_mx(
                out=codes[:, c0:c1].bitcast(FP8X4),
                scales=scales[:, c0:c1],
                in_=grouped[:, 4 * c0 : 4 * c1],
            )

        x_sb = load(xf, const, "x_sb", 4)
        w_sb = {}
        for c in range(AHEAD):
            w_sb[c] = load_chunk(c)

        x_banks = [transposes(x_sb, 2 * b, 2) for b in range(4)]
        x_grouped = grp.tile([P, K], BF16, name="grouped", align_bytes=64)
        x_codes = const.tile([P, PASSES * P], U32, name="x_codes", align_bytes=64)
        x_scales = const.tile([P, PASSES * P], U8, name="x_scales", align_bytes=64)
        regroup(nc.scalar.copy, x_banks[0], x_grouped, 0, 2)
        regroup(nc.vector.tensor_copy, x_banks[1], x_grouped, 2, 2)
        regroup(nc.scalar.copy, x_banks[2], x_grouped, 4, 2)
        regroup(nc.vector.tensor_copy, x_banks[3], x_grouped, 6, 2)
        quantise(x_grouped, x_codes, x_scales, 0, 4)
        quantise(x_grouped, x_codes, x_scales, 4, 4)

        w_q = {}
        acc = {}
        late = []

        def multiply(m):
            if m % 4 == 0 or m == LAST:
                acc[m] = aps.tile([P, 512], F32, name="acc")
                dst = acc[m][:, 0:P]
            else:
                dst = acc[m - m % 4][:, (m % 4) * P : (m % 4 + 1) * P]
            codes, scales = w_q[m]
            for g in range(PASSES):
                s = slice(g * P, (g + 1) * P)
                nc.tensor.matmul_mx(
                    out=dst,
                    lhsT=x_codes[:, s].bitcast(FP8X4),
                    lhsT_scale=x_scales[:, s],
                    rhs=codes[:, s].bitcast(FP8X4),
                    rhs_scale=scales[:, s],
                    start=(g == 0),
                    stop=(g == PASSES - 1),
                )

        def finish(first, count):
            cols = slice(first * P, (first + count) * P)
            nc.scalar.copy(out=o_sb[:, cols], in_=acc[first][:, 0 : count * P])
            if first // 4 < LATE_FROM:
                nc.scalar.dma_start(out=of[:, cols], in_=o_sb[:, cols])
            else:
                late.append(cols)

        loaded = AHEAD
        multiplied = 0
        sent = 0
        for c in range(CHUNKS):
            if c < LAST:
                banks = [transposes(w_sb[c], 2 * b, 2) for b in range(4)]
            else:
                banks = [transposes(w_sb[c], 2 * b, 2) for b in range(3)]
                banks.append(transposes(w_sb[c], 6, 1))
                banks.append(transposes(w_sb[c], 7, 1))
            if loaded < CHUNKS:
                w_sb[loaded] = load_chunk(loaded)
                loaded += 1
            done = list(range(multiplied, c if c >= LAST - 1 else c - LAG + 1))
            for m in done:
                multiply(m)
            multiplied += len(done)
            grouped = grp.tile([P, K], BF16, name="grouped", align_bytes=64)
            codes = qnt.tile([P, PASSES * P], U32, name="codes", align_bytes=64)
            scales = qnt.tile([P, PASSES * P], U8, name="scales", align_bytes=64)
            w_q[c] = (codes, scales)
            if c < LAST:
                regroup(nc.scalar.copy, banks[0], grouped, 0, 2)
                regroup(nc.scalar.copy, banks[1], grouped, 2, 2)
                regroup(nc.scalar.copy, banks[2], grouped, 4, 2)
                regroup(nc.vector.tensor_copy, banks[3], grouped, 6, 2)
                quantise(grouped, codes, scales, 0, 4)
                quantise(grouped, codes, scales, 4, 4)
            else:
                regroup(nc.scalar.copy, banks[0], grouped, 0, 2)
                regroup(nc.vector.tensor_copy, banks[1], grouped, 2, 2)
                regroup(nc.scalar.copy, banks[2], grouped, 4, 2)
                quantise(grouped, codes, scales, 0, 2)
                quantise(grouped, codes, scales, 2, 2)
                regroup(nc.scalar.copy, banks[3], grouped, 6, 1)
                regroup(nc.vector.tensor_copy, banks[4], grouped, 7, 1)
                quantise(grouped, codes, scales, 4, 2)
                quantise(grouped, codes, scales, 6, 2)
            for m in done:
                if m % 4 == 3:
                    finish(m - 3, 4)
                elif m == LAST - 1:
                    finish(m - 2, 3)
            if loaded == CHUNKS:
                for cols in late[sent:]:
                    nc.sync.dma_start(out=of[:, cols], in_=o_sb[:, cols])
                sent = len(late)
        multiply(LAST)
        finish(LAST, 1)
        for cols in late[sent:]:
            nc.sync.dma_start(out=of[:, cols], in_=o_sb[:, cols])
